import numpy as np
import ml_dtypes

BF16 = ml_dtypes.bfloat16


def bf(x):
    return np.asarray(x, np.float32).astype(BF16)


def f32(x):
    return np.asarray(x, np.float32)


def f64(x):
    return np.asarray(x).astype(np.float64)


def striped(idx):
    return np.tile(idx.reshape(-1, 16).T, (8, 1))


C, S, T, M, K, N = 512, 256, 64, 16, 4, 1024


def setup_inputs():
    return {"text_table": f32(np.random.standard_normal((C, S))), "type_emb": f32(np.random.standard_normal((C, N))), "queries": f32(np.random.standard_normal((C, T))), "output_mask": f32(1.0 + 0.1 * np.random.standard_normal((1, T))), "offs": striped(np.concatenate([np.random.permutation(S) for _ in range(K)]))}


def reference(text_table, type_emb, queries, output_mask, offs):
    idx = offs[:16].T.reshape(-1)
    q = f64(queries)
    e = (f64(text_table)[:, idx] + f64(type_emb)).reshape(C, T, M)
    s = (e * q[:, :, None]).sum(axis=0) / np.sqrt(C)
    p = np.exp(s - s.max(axis=1, keepdims=True))
    p = p / p.sum(axis=1, keepdims=True)
    att = (e * p[None, :, :]).sum(axis=2)
    return att * f64(output_mask) + q

@@ -1,0 +1,109 @@
+import math
+
+import concourse.mybir as mybir
+
+F32 = mybir.dt.float32
+BF16 = mybir.dt.bfloat16
+U16 = mybir.dt.uint16
+ADD = mybir.AluOpType.add
+SUBTRACT = mybir.AluOpType.subtract
+MULT = mybir.AluOpType.mult
+EXP = mybir.ActivationFunctionType.Exp
+X = mybir.AxisListType.X
+
+P = 128
+C, S, T, M = 512, 256, 64, 16
+N = T * M
+BLOCKS = C // P
+PIECE = 256
+PIECES = N // PIECE
+TOKENS = PIECE // M
+
+FLOPS = 4 * C * N
+
+
+def tile_dependencymemory_kernel(tc, text_table, type_emb, queries, output_mask, offs, out):
+    nc = tc.nc
+    type_blocks = type_emb.rearrange("(b p) n -> p b n", p=P)
+    with (
+        tc.tile_pool(name="held", bufs=1) as held,
+        tc.tile_pool(name="work", bufs=2) as work,
+        tc.psum_pool(name="psum", bufs=2) as psum,
+    ):
+        offsets = held.tile([P, N // 16], U16, name="offsets")
+        nc.sync.dma_start(offsets[:], offs)
+        tables = [held.tile([P, S], F32, name=f"table{b}") for b in range(BLOCKS)]
+        for b in range(BLOCKS):
+            nc.sync.dma_start(tables[b][:], text_table[b * P : (b + 1) * P, :])
+        query = held.tile([P, BLOCKS, T], F32, name="query")
+        nc.scalar.dma_start(query[:], queries.rearrange("(b p) t -> p b t", p=P))
+        mask = held.tile([P, T], F32, name="mask")
+        nc.scalar.dma_start(mask[:], output_mask.rearrange("o t -> (o t)").partition_broadcast(P))
+        types = [held.tile([P, BLOCKS, PIECE], F32, name=f"types{k}") for k in range(PIECES)]
+        for k in range(PIECES):
+            for b in range(BLOCKS):
+                queue = nc.sync if b % 2 == 0 else nc.scalar
+                queue.dma_start(types[k][:, b, :], type_blocks[:, b, k * PIECE : (k + 1) * PIECE])
+
+        ones = held.tile([P, P], BF16, name="ones")
+        nc.gpsimd.memset(ones[:], 1.0)
+        result = held.tile([P, BLOCKS, T], F32, name="result")
+
+        for k in range(PIECES):
+            tokens = slice(k * TOKENS, (k + 1) * TOKENS)
+            query_k = query[:, :, tokens]
+
+            slots = work.tile([P, BLOCKS, PIECE], F32, name="slots")
+            piece_offsets = offsets[:, k * (PIECE // 16) : (k + 1) * (PIECE // 16)]
+            for b in range(BLOCKS):
+                nc.vector.tensor_tensor(
+                    slots[:, b, :], tables[b][:].indirect(piece_offsets), types[k][:, b, :], ADD
+                )
+            slots_by_token = slots[:].rearrange("p b (t m) -> p b t m", m=M)
+
+            products = work.tile([P, BLOCKS, PIECE], BF16, name="products")
+            nc.vector.tensor_tensor(
+                products[:].rearrange("p b (t m) -> p b t m", m=M),
+                slots_by_token,
+                query_k.unsqueeze(3).to_broadcast([P, BLOCKS, TOKENS, M]),
+                MULT,
+            )
+            scores = psum.tile([P, TOKENS, M], F32, name="scores")
+            for b in range(BLOCKS):
+                nc.tensor.matmul(
+                    scores[:].rearrange("p t m -> p (t m)"),
+                    ones[:],
+                    products[:, b, :],
+                    start=(b == 0),
+                    stop=(b == BLOCKS - 1),
+                )
+
+            top = work.tile([P, TOKENS], F32, name="top")
+            nc.vector.reduce_max(top[:], scores[:], axis=X)
+            shifted = work.tile([P, TOKENS, M], F32, name="shifted")
+            nc.vector.tensor_tensor(
+                shifted[:], scores[:], top[:].unsqueeze(2).to_broadcast([P, TOKENS, M]), SUBTRACT
+            )
+            weights = work.tile([P, TOKENS, M], F32, name="weights")
+            nc.scalar.activation(weights[:], shifted[:], EXP, scale=1.0 / math.sqrt(C))
+            total = work.tile([P, TOKENS], F32, name="total")
+            nc.vector.reduce_sum(total[:], weights[:], axis=X)
+            gain = work.tile([P, TOKENS], F32, name="gain")
+            nc.vector.reciprocal(gain[:], total[:])
+            nc.vector.tensor_tensor(gain[:], gain[:], mask[:, tokens], MULT)
+
+            weighted = work.tile([P, BLOCKS, TOKENS, M], F32, name="weighted")
+            nc.vector.tensor_tensor(
+                weighted[:],
+                slots_by_token,
+                weights[:].unsqueeze(1).to_broadcast([P, BLOCKS, TOKENS, M]),
+                MULT,
+            )
+            attended = work.tile([P, BLOCKS, TOKENS], F32, name="attended")
+            nc.vector.reduce_sum(attended[:], weighted[:], axis=X)
+            nc.vector.tensor_tensor(
+                attended[:], attended[:], gain[:].unsqueeze(1).to_broadcast([P, BLOCKS, TOKENS]), MULT
+            )
+            nc.vector.tensor_tensor(result[:, :, tokens], attended[:], query_k, ADD)
+
+        nc.sync.dma_start(out.rearrange("(b p) t -> p b t", p=P), result[:])

@@ -1,13 +1,14 @@
 import math
 
 import concourse.mybir as mybir
+from concourse.masks import make_identity
 
 F32 = mybir.dt.float32
-BF16 = mybir.dt.bfloat16
 U16 = mybir.dt.uint16
 ADD = mybir.AluOpType.add
-SUBTRACT = mybir.AluOpType.subtract
 MULT = mybir.AluOpType.mult
+IS_GE = mybir.AluOpType.is_ge
+NOT_EQUAL = mybir.AluOpType.not_equal
 EXP = mybir.ActivationFunctionType.Exp
 X = mybir.AxisListType.X
 
@@ -17,7 +18,10 @@ N = T * M
 BLOCKS = C // P
 PIECE = 256
 PIECES = N // PIECE
+HALVES = PIECE // P
 TOKENS = PIECE // M
+OWN = P // M
+FAR = -1.0e30
 
 FLOPS = 4 * C * N
 
@@ -27,83 +31,129 @@ def tile_dependencymemory_kernel(tc, text_table, type_emb, queries, output_mask,
     type_blocks = type_emb.rearrange("(b p) n -> p b n", p=P)
     with (
         tc.tile_pool(name="held", bufs=1) as held,
-        tc.tile_pool(name="work", bufs=2) as work,
-        tc.psum_pool(name="psum", bufs=2) as psum,
+        tc.tile_pool(name="work", bufs=3) as work,
+        tc.psum_pool(name="twice", bufs=2) as twice,
+        tc.psum_pool(name="once", bufs=1) as once,
     ):
         offsets = held.tile([P, N // 16], U16, name="offsets")
         nc.sync.dma_start(offsets[:], offs)
-        tables = [held.tile([P, S], F32, name=f"table{b}") for b in range(BLOCKS)]
-        for b in range(BLOCKS):
-            nc.sync.dma_start(tables[b][:], text_table[b * P : (b + 1) * P, :])
         query = held.tile([P, BLOCKS, T], F32, name="query")
         nc.scalar.dma_start(query[:], queries.rearrange("(b p) t -> p b t", p=P))
+        tables = [held.tile([P, S], F32, name=f"table{b}") for b in range(BLOCKS)]
+        types = [held.tile([P, BLOCKS, PIECE], F32, name=f"types{k}") for k in range(PIECES)]
+        for b in range(BLOCKS):
+            nc.sync.dma_start(tables[b][:], text_table[b * P : (b + 1) * P, :])
+            nc.scalar.dma_start(types[0][:, b, :], type_blocks[:, b, 0:PIECE])
         mask = held.tile([P, T], F32, name="mask")
         nc.scalar.dma_start(mask[:], output_mask.rearrange("o t -> (o t)").partition_broadcast(P))
-        types = [held.tile([P, BLOCKS, PIECE], F32, name=f"types{k}") for k in range(PIECES)]
-        for k in range(PIECES):
+        for k in range(1, PIECES):
             for b in range(BLOCKS):
                 queue = nc.sync if b % 2 == 0 else nc.scalar
                 queue.dma_start(types[k][:, b, :], type_blocks[:, b, k * PIECE : (k + 1) * PIECE])
 
-        ones = held.tile([P, P], BF16, name="ones")
-        nc.gpsimd.memset(ones[:], 1.0)
+        identity = held.tile([P, P], F32, name="identity")
+        make_identity(nc, identity[:])
+        away = held.tile([P, N // P, T], F32, name="away")
+        nc.gpsimd.memset(away[:], 0.0)
+        nc.gpsimd.affine_select(
+            out=away[:], in_=away[:], compare_op=IS_GE, fill=FAR,
+            base=0, channel_multiplier=1, pattern=[[P, N // P], [-M, T]],
+        )
+        nc.gpsimd.affine_select(
+            out=away[:], in_=away[:], compare_op=IS_GE, fill=FAR,
+            base=M - 1, channel_multiplier=-1, pattern=[[-P, N // P], [M, T]],
+        )
+        pick = held.tile([P, PIECES, HALVES, OWN], F32, name="pick")
+        nc.gpsimd.memset(pick[:], 0.0)
+        nc.gpsimd.affine_select(
+            out=pick[:], in_=pick[:], compare_op=NOT_EQUAL, fill=1.0,
+            base=0, channel_multiplier=1, pattern=[[-TOKENS, PIECES], [-(T + OWN), HALVES], [-1, OWN]],
+        )
+        query_scaled = held.tile([P, BLOCKS, T], F32, name="query_scaled")
+        nc.scalar.mul(query_scaled[:], query[:], 1.0 / math.sqrt(C))
         result = held.tile([P, BLOCKS, T], F32, name="result")
 
-        for k in range(PIECES):
-            tokens = slice(k * TOKENS, (k + 1) * TOKENS)
-            query_k = query[:, :, tokens]
+        slots, scores, flipped, rows, weights, total, shares_psum, shares, attended = (
+            {}, {}, {}, {}, {}, {}, {}, {}, {},
+        )
 
-            slots = work.tile([P, BLOCKS, PIECE], F32, name="slots")
-            piece_offsets = offsets[:, k * (PIECE // 16) : (k + 1) * (PIECE // 16)]
-            for b in range(BLOCKS):
-                nc.vector.tensor_tensor(
-                    slots[:, b, :], tables[b][:].indirect(piece_offsets), types[k][:, b, :], ADD
-                )
-            slots_by_token = slots[:].rearrange("p b (t m) -> p b t m", m=M)
-
-            products = work.tile([P, BLOCKS, PIECE], BF16, name="products")
+        def look_up(k, b):
+            if b == 0:
+                slots[k] = work.tile([P, BLOCKS, PIECE], F32, name="slots")
+                scores[k] = twice.tile([P, HALVES, T], F32, name="scores")
+                flipped[k] = work.tile([P, HALVES, C], F32, name="flipped")
             nc.vector.tensor_tensor(
-                products[:].rearrange("p b (t m) -> p b t m", m=M),
-                slots_by_token,
-                query_k.unsqueeze(3).to_broadcast([P, BLOCKS, TOKENS, M]),
-                MULT,
+                slots[k][:, b, :],
+                tables[b][:].indirect(offsets[:, k * (PIECE // 16) : (k + 1) * (PIECE // 16)]),
+                types[k][:, b, :],
+                ADD,
             )
-            scores = psum.tile([P, TOKENS, M], F32, name="scores")
-            for b in range(BLOCKS):
+            for h in range(HALVES):
                 nc.tensor.matmul(
-                    scores[:].rearrange("p t m -> p (t m)"),
-                    ones[:],
-                    products[:, b, :],
-                    start=(b == 0),
-                    stop=(b == BLOCKS - 1),
+                    scores[k][:, h, :],
+                    slots[k][:, b, h * P : (h + 1) * P],
+                    query_scaled[:, b, :],
+                    start=(b == 0 and h == 0),
+                    stop=(b == BLOCKS - 1 and h == HALVES - 1),
                 )
+            flips = twice.tile([P, HALVES, P], F32, name="flips")
+            for h in range(HALVES):
+                nc.tensor.transpose(flips[:, h, :], slots[k][:, b, h * P : (h + 1) * P], identity[:])
+            nc.scalar.copy(flipped[k][:, :, b * P : (b + 1) * P], flips[:])
 
-            top = work.tile([P, TOKENS], F32, name="top")
-            nc.vector.reduce_max(top[:], scores[:], axis=X)
-            shifted = work.tile([P, TOKENS, M], F32, name="shifted")
-            nc.vector.tensor_tensor(
-                shifted[:], scores[:], top[:].unsqueeze(2).to_broadcast([P, TOKENS, M]), SUBTRACT
-            )
-            weights = work.tile([P, TOKENS, M], F32, name="weights")
-            nc.scalar.activation(weights[:], shifted[:], EXP, scale=1.0 / math.sqrt(C))
-            total = work.tile([P, TOKENS], F32, name="total")
-            nc.vector.reduce_sum(total[:], weights[:], axis=X)
-            gain = work.tile([P, TOKENS], F32, name="gain")
-            nc.vector.reciprocal(gain[:], total[:])
-            nc.vector.tensor_tensor(gain[:], gain[:], mask[:, tokens], MULT)
 
-            weighted = work.tile([P, BLOCKS, TOKENS, M], F32, name="weighted")
+        def flip_scores(k):
+            masked = work.tile([P, HALVES, T], F32, name="masked")
+            nc.vector.tensor_tensor(masked[:], scores[k][:], away[:, k * HALVES : (k + 1) * HALVES, :], ADD)
+            rows[k] = once.tile([P, P], F32, name="rows")
+            nc.tensor.transpose(rows[k][:], masked[:].rearrange("p h t -> p (h t)"), identity[:])
+
+        def exponentials(k):
+            minus_top = work.tile([P, 1], F32, name="minus_top")
+            nc.vector.reduce_max(minus_top[:], rows[k][:], axis=X, negate=True)
+            weights[k] = work.tile([P, P], F32, name="weights")
+            total[k] = work.tile([P, 1], F32, name="total")
+            nc.scalar.activation(weights[k][:], rows[k][:], EXP, bias=minus_top[:], accum_out=total[k][:])
+
+        def flip_back(k):
+            inverse = work.tile([P, 1], F32, name="inverse")
+            nc.vector.reciprocal(inverse[:], total[k][:])
+            chosen = work.tile([P, TOKENS], F32, name="chosen")
+            nc.vector.tensor_scalar_mul(chosen[:], pick[:, k, :, :].rearrange("p h i -> p (h i)"), inverse[:])
+            shares_psum[k] = once.tile([P, TOKENS], F32, name="shares_psum")
+            nc.tensor.matmul(shares_psum[k][:], weights[k][:], chosen[:], start=True, stop=True)
+
+        def apply_mask(k):
+            shares[k] = work.tile([P, TOKENS], F32, name="shares")
             nc.vector.tensor_tensor(
-                weighted[:],
-                slots_by_token,
-                weights[:].unsqueeze(1).to_broadcast([P, BLOCKS, TOKENS, M]),
-                MULT,
+                shares[k][:], shares_psum[k][:], mask[:, k * TOKENS : (k + 1) * TOKENS], MULT
             )
-            attended = work.tile([P, BLOCKS, TOKENS], F32, name="attended")
-            nc.vector.reduce_sum(attended[:], weighted[:], axis=X)
-            nc.vector.tensor_tensor(
-                attended[:], attended[:], gain[:].unsqueeze(1).to_broadcast([P, BLOCKS, TOKENS]), MULT
-            )
-            nc.vector.tensor_tensor(result[:, :, tokens], attended[:], query_k, ADD)
+
+        softmax_steps = [flip_scores, exponentials, flip_back, apply_mask]
+
+        def attend(k, b):
+            tokens = slice(k * TOKENS, (k + 1) * TOKENS)
+            if b == 0:
+                attended[k] = twice.tile([P, BLOCKS, TOKENS], F32, name="attended")
+                nc.tensor.matmul(attended[k][:], identity[:], query[:, :, tokens], start=True, stop=False)
+            for h in range(HALVES):
+                nc.tensor.matmul(
+                    attended[k][:, b, h * OWN : (h + 1) * OWN],
+                    flipped[k][:, h, b * P : (b + 1) * P],
+                    shares[k][:, h * OWN : (h + 1) * OWN],
+                    start=False,
+                    stop=(b == BLOCKS - 1 and h == HALVES - 1),
+                )
+            if b == BLOCKS - 1:
+                nc.scalar.copy(result[:, :, tokens], attended[k][:])
+
+        for k in range(PIECES + 2):
+            for b in range(BLOCKS):
+                if k < PIECES:
+                    look_up(k, b)
+                if 1 <= k <= PIECES:
+                    softmax_steps[b](k - 1)
+                if k >= 2:
+                    attend(k - 2, b)
 
         nc.sync.dma_start(out.rearrange("(b p) t -> p b t", p=P), result[:])

@@ -4,11 +4,11 @@ import concourse.mybir as mybir
 from concourse.masks import make_identity
 
 F32 = mybir.dt.float32
+BF16 = mybir.dt.bfloat16
 U16 = mybir.dt.uint16
 ADD = mybir.AluOpType.add
 MULT = mybir.AluOpType.mult
 IS_GE = mybir.AluOpType.is_ge
-NOT_EQUAL = mybir.AluOpType.not_equal
 EXP = mybir.ActivationFunctionType.Exp
 X = mybir.AxisListType.X
 
@@ -18,9 +18,7 @@ N = T * M
 BLOCKS = C // P
 PIECE = 256
 PIECES = N // PIECE
-HALVES = PIECE // P
 TOKENS = PIECE // M
-OWN = P // M
 FAR = -1.0e30
 
 FLOPS = 4 * C * N
@@ -31,9 +29,9 @@ def tile_dependencymemory_kernel(tc, text_table, type_emb, queries, output_mask,
     type_blocks = type_emb.rearrange("(b p) n -> p b n", p=P)
     with (
         tc.tile_pool(name="held", bufs=1) as held,
-        tc.tile_pool(name="work", bufs=3) as work,
-        tc.psum_pool(name="twice", bufs=2) as twice,
-        tc.psum_pool(name="once", bufs=1) as once,
+        tc.tile_pool(name="work", bufs=2) as work,
+        tc.tile_pool(name="kept", bufs=PIECES) as kept,
+        tc.psum_pool(name="psum", bufs=2) as psum,
     ):
         offsets = held.tile([P, N // 16], U16, name="offsets")
         nc.sync.dma_start(offsets[:], offs)
@@ -51,109 +49,86 @@ def tile_dependencymemory_kernel(tc, text_table, type_emb, queries, output_mask,
                 queue = nc.sync if b % 2 == 0 else nc.scalar
                 queue.dma_start(types[k][:, b, :], type_blocks[:, b, k * PIECE : (k + 1) * PIECE])
 
-        identity = held.tile([P, P], F32, name="identity")
+        identity = held.tile([P, P], BF16, name="identity")
         make_identity(nc, identity[:])
-        away = held.tile([P, N // P, T], F32, name="away")
-        nc.gpsimd.memset(away[:], 0.0)
+        away_wide = held.tile([P, PIECE], F32, name="away_wide")
+        nc.gpsimd.memset(away_wide[:], 0.0)
         nc.gpsimd.affine_select(
-            out=away[:], in_=away[:], compare_op=IS_GE, fill=FAR,
-            base=0, channel_multiplier=1, pattern=[[P, N // P], [-M, T]],
+            out=away_wide[:], in_=away_wide[:], compare_op=IS_GE, fill=FAR,
+            base=0, channel_multiplier=-M, pattern=[[1, PIECE]],
         )
         nc.gpsimd.affine_select(
-            out=away[:], in_=away[:], compare_op=IS_GE, fill=FAR,
-            base=M - 1, channel_multiplier=-1, pattern=[[-P, N // P], [M, T]],
+            out=away_wide[:], in_=away_wide[:], compare_op=IS_GE, fill=FAR,
+            base=M - 1, channel_multiplier=M, pattern=[[-1, PIECE]],
         )
-        pick = held.tile([P, PIECES, HALVES, OWN], F32, name="pick")
-        nc.gpsimd.memset(pick[:], 0.0)
-        nc.gpsimd.affine_select(
-            out=pick[:], in_=pick[:], compare_op=NOT_EQUAL, fill=1.0,
-            base=0, channel_multiplier=1, pattern=[[-TOKENS, PIECES], [-(T + OWN), HALVES], [-1, OWN]],
-        )
+        away = held.tile([P, PIECE], BF16, name="away")
+        nc.vector.tensor_copy(away[:], away_wide[:])
+        ones = held.tile([TOKENS, P], F32, name="ones")
+        nc.gpsimd.memset(ones[:], 1.0)
         query_scaled = held.tile([P, BLOCKS, T], F32, name="query_scaled")
         nc.scalar.mul(query_scaled[:], query[:], 1.0 / math.sqrt(C))
         result = held.tile([P, BLOCKS, T], F32, name="result")
 
-        slots, scores, flipped, rows, weights, total, shares_psum, shares, attended = (
-            {}, {}, {}, {}, {}, {}, {}, {}, {},
-        )
+        slots, scores, weights, total, shares = {}, {}, {}, {}, {}
 
-        def look_up(k, b):
-            if b == 0:
-                slots[k] = work.tile([P, BLOCKS, PIECE], F32, name="slots")
-                scores[k] = twice.tile([P, HALVES, T], F32, name="scores")
-                flipped[k] = work.tile([P, HALVES, C], F32, name="flipped")
-            nc.vector.tensor_tensor(
-                slots[k][:, b, :],
-                tables[b][:].indirect(offsets[:, k * (PIECE // 16) : (k + 1) * (PIECE // 16)]),
-                types[k][:, b, :],
-                ADD,
-            )
-            for h in range(HALVES):
-                nc.tensor.matmul(
-                    scores[k][:, h, :],
-                    slots[k][:, b, h * P : (h + 1) * P],
-                    query_scaled[:, b, :],
-                    start=(b == 0 and h == 0),
-                    stop=(b == BLOCKS - 1 and h == HALVES - 1),
+        def look_up(k):
+            slots[k] = kept.tile([P, BLOCKS, PIECE], F32, name="slots")
+            scores[k] = psum.tile([TOKENS, PIECE], F32, name="scores")
+            nc.tensor.matmul(scores[k][:], identity[:, 0:TOKENS], away[:], start=True, stop=False)
+            for b in range(BLOCKS):
+                nc.vector.tensor_tensor(
+                    slots[k][:, b, :],
+                    tables[b][:].indirect(offsets[:, k * (PIECE // 16) : (k + 1) * (PIECE // 16)]),
+                    types[k][:, b, :],
+                    ADD,
                 )
-            flips = twice.tile([P, HALVES, P], F32, name="flips")
-            for h in range(HALVES):
-                nc.tensor.transpose(flips[:, h, :], slots[k][:, b, h * P : (h + 1) * P], identity[:])
-            nc.scalar.copy(flipped[k][:, :, b * P : (b + 1) * P], flips[:])
-
-
-        def flip_scores(k):
-            masked = work.tile([P, HALVES, T], F32, name="masked")
-            nc.vector.tensor_tensor(masked[:], scores[k][:], away[:, k * HALVES : (k + 1) * HALVES, :], ADD)
-            rows[k] = once.tile([P, P], F32, name="rows")
-            nc.tensor.transpose(rows[k][:], masked[:].rearrange("p h t -> p (h t)"), identity[:])
+                nc.tensor.matmul(
+                    scores[k][:],
+                    query_scaled[:, b, k * TOKENS : (k + 1) * TOKENS],
+                    slots[k][:, b, :],
+                    start=False,
+                    stop=(b == BLOCKS - 1),
+                )
 
         def exponentials(k):
-            minus_top = work.tile([P, 1], F32, name="minus_top")
-            nc.vector.reduce_max(minus_top[:], rows[k][:], axis=X, negate=True)
-            weights[k] = work.tile([P, P], F32, name="weights")
-            total[k] = work.tile([P, 1], F32, name="total")
-            nc.scalar.activation(weights[k][:], rows[k][:], EXP, bias=minus_top[:], accum_out=total[k][:])
+            minus_top = work.tile([TOKENS, 1], F32, name="minus_top")
+            nc.vector.reduce_max(minus_top[:], scores[k][:], axis=X, negate=True)
+            weights[k] = work.tile([TOKENS, PIECE], F32, name="weights")
+            total[k] = work.tile([TOKENS, 1], F32, name="total")
+            nc.scalar.activation(weights[k][:], scores[k][:], EXP, bias=minus_top[:], accum_out=total[k][:])
 
-        def flip_back(k):
-            inverse = work.tile([P, 1], F32, name="inverse")
+        def spread(k):
+            inverse = work.tile([TOKENS, 1], F32, name="inverse")
             nc.vector.reciprocal(inverse[:], total[k][:])
-            chosen = work.tile([P, TOKENS], F32, name="chosen")
-            nc.vector.tensor_scalar_mul(chosen[:], pick[:, k, :, :].rearrange("p h i -> p (h i)"), inverse[:])
-            shares_psum[k] = once.tile([P, TOKENS], F32, name="shares_psum")
-            nc.tensor.matmul(shares_psum[k][:], weights[k][:], chosen[:], start=True, stop=True)
+            divide = work.tile([TOKENS, P], F32, name="divide")
+            nc.vector.tensor_scalar_mul(divide[:], ones[:], inverse[:])
+            shares[k] = psum.tile([P, PIECE], F32, name="shares")
+            nc.tensor.matmul(shares[k][:], divide[:], weights[k][:], start=True, stop=True)
 
-        def apply_mask(k):
-            shares[k] = work.tile([P, TOKENS], F32, name="shares")
-            nc.vector.tensor_tensor(
-                shares[k][:], shares_psum[k][:], mask[:, k * TOKENS : (k + 1) * TOKENS], MULT
-            )
-
-        softmax_steps = [flip_scores, exponentials, flip_back, apply_mask]
-
-        def attend(k, b):
+        def attend(k):
             tokens = slice(k * TOKENS, (k + 1) * TOKENS)
-            if b == 0:
-                attended[k] = twice.tile([P, BLOCKS, TOKENS], F32, name="attended")
-                nc.tensor.matmul(attended[k][:], identity[:], query[:, :, tokens], start=True, stop=False)
-            for h in range(HALVES):
-                nc.tensor.matmul(
-                    attended[k][:, b, h * OWN : (h + 1) * OWN],
-                    flipped[k][:, h, b * P : (b + 1) * P],
-                    shares[k][:, h * OWN : (h + 1) * OWN],
-                    start=False,
-                    stop=(b == BLOCKS - 1 and h == HALVES - 1),
-                )
-            if b == BLOCKS - 1:
-                nc.scalar.copy(result[:, :, tokens], attended[k][:])
+            weighted = work.tile([P, BLOCKS, TOKENS, M], F32, name="weighted")
+            nc.vector.tensor_tensor(
+                weighted[:].rearrange("p b t m -> p b (t m)"),
+                slots[k][:],
+                shares[k][:].unsqueeze(1).to_broadcast([P, BLOCKS, PIECE]),
+                MULT,
+            )
+            attended = work.tile([P, BLOCKS, TOKENS], F32, name="attended")
+            nc.vector.reduce_sum(attended[:], weighted[:], axis=X)
+            nc.vector.tensor_tensor(
+                attended[:], attended[:], mask[:, tokens].unsqueeze(1).to_broadcast([P, BLOCKS, TOKENS]), MULT
+            )
+            nc.vector.tensor_tensor(result[:, :, tokens], attended[:], query[:, :, tokens], ADD)
 
-        for k in range(PIECES + 2):
-            for b in range(BLOCKS):
-                if k < PIECES:
-                    look_up(k, b)
-                if 1 <= k <= PIECES:
-                    softmax_steps[b](k - 1)
-                if k >= 2:
-                    attend(k - 2, b)
+        for k in range(PIECES + 3):
+            if k < PIECES:
+                look_up(k)
+            if 0 <= k - 2 < PIECES:
+                spread(k - 2)
+            if 0 <= k - 3 < PIECES:
+                attend(k - 3)
+            if 0 <= k - 1 < PIECES:
+                exponentials(k - 1)
 
         nc.sync.dma_start(out.rearrange("(b p) t -> p b t", p=P), result[:])

@@ -32,6 +32,7 @@ def tile_dependencymemory_kernel(tc, text_table, type_emb, queries, output_mask,
         tc.tile_pool(name="work", bufs=2) as work,
         tc.tile_pool(name="kept", bufs=PIECES) as kept,
         tc.psum_pool(name="psum", bufs=2) as psum,
+        tc.psum_pool(name="kept_psum", bufs=PIECES) as kept_psum,
     ):
         offsets = held.tile([P, N // 16], U16, name="offsets")
         nc.sync.dma_start(offsets[:], offs)
@@ -62,7 +63,7 @@ def tile_dependencymemory_kernel(tc, text_table, type_emb, queries, output_mask,
             base=M - 1, channel_multiplier=M, pattern=[[-1, PIECE]],
         )
         away = held.tile([P, PIECE], BF16, name="away")
-        nc.vector.tensor_copy(away[:], away_wide[:])
+        nc.gpsimd.tensor_copy(away[:], away_wide[:])
         ones = held.tile([TOKENS, P], F32, name="ones")
         nc.gpsimd.memset(ones[:], 1.0)
         query_scaled = held.tile([P, BLOCKS, T], F32, name="query_scaled")
@@ -102,7 +103,7 @@ def tile_dependencymemory_kernel(tc, text_table, type_emb, queries, output_mask,
             nc.vector.reciprocal(inverse[:], total[k][:])
             divide = work.tile([TOKENS, P], F32, name="divide")
             nc.vector.tensor_scalar_mul(divide[:], ones[:], inverse[:])
-            shares[k] = psum.tile([P, PIECE], F32, name="shares")
+            shares[k] = kept_psum.tile([P, PIECE], F32, name="shares")
             nc.tensor.matmul(shares[k][:], divide[:], weights[k][:], start=True, stop=True)
 
         def attend(k):
@@ -121,14 +122,14 @@ def tile_dependencymemory_kernel(tc, text_table, type_emb, queries, output_mask,
             )
             nc.vector.tensor_tensor(result[:, :, tokens], attended[:], query[:, :, tokens], ADD)
 
-        for k in range(PIECES + 3):
+        for k in range(PIECES + 2):
             if k < PIECES:
                 look_up(k)
-            if 0 <= k - 2 < PIECES:
-                spread(k - 2)
-            if 0 <= k - 3 < PIECES:
-                attend(k - 3)
             if 0 <= k - 1 < PIECES:
                 exponentials(k - 1)
+            if 0 <= k - 2 < PIECES:
+                spread(k - 2)
+        for k in range(PIECES):
+            attend(k)
 
         nc.sync.dma_start(out.rearrange("(b p) t -> p b t", p=P), result[:])

@@ -37,18 +37,17 @@ def tile_dependencymemory_kernel(tc, text_table, type_emb, queries, output_mask,
         offsets = held.tile([P, N // 16], U16, name="offsets")
         nc.sync.dma_start(offsets[:], offs)
         query = held.tile([P, BLOCKS, T], F32, name="query")
-        nc.scalar.dma_start(query[:], queries.rearrange("(b p) t -> p b t", p=P))
+        nc.sync.dma_start(query[:], queries.rearrange("(b p) t -> p b t", p=P))
         tables = [held.tile([P, S], F32, name=f"table{b}") for b in range(BLOCKS)]
         types = [held.tile([P, BLOCKS, PIECE], F32, name=f"types{k}") for k in range(PIECES)]
         for b in range(BLOCKS):
             nc.sync.dma_start(tables[b][:], text_table[b * P : (b + 1) * P, :])
-            nc.scalar.dma_start(types[0][:, b, :], type_blocks[:, b, 0:PIECE])
+            nc.sync.dma_start(types[0][:, b, :], type_blocks[:, b, 0:PIECE])
         mask = held.tile([P, T], F32, name="mask")
-        nc.scalar.dma_start(mask[:], output_mask.rearrange("o t -> (o t)").partition_broadcast(P))
+        nc.sync.dma_start(mask[:], output_mask.rearrange("o t -> (o t)").partition_broadcast(P))
         for k in range(1, PIECES):
             for b in range(BLOCKS):
-                queue = nc.sync if b % 2 == 0 else nc.scalar
-                queue.dma_start(types[k][:, b, :], type_blocks[:, b, k * PIECE : (k + 1) * PIECE])
+                nc.sync.dma_start(types[k][:, b, :], type_blocks[:, b, k * PIECE : (k + 1) * PIECE])
 
         identity = held.tile([P, P], BF16, name="identity")
         make_identity(nc, identity[:])
@@ -67,7 +66,7 @@ def tile_dependencymemory_kernel(tc, text_table, type_emb, queries, output_mask,
         ones = held.tile([TOKENS, P], F32, name="ones")
         nc.gpsimd.memset(ones[:], 1.0)
         query_scaled = held.tile([P, BLOCKS, T], F32, name="query_scaled")
-        nc.scalar.mul(query_scaled[:], query[:], 1.0 / math.sqrt(C))
+        nc.vector.tensor_scalar_mul(query_scaled[:], query[:], 1.0 / math.sqrt(C))
         result = held.tile([P, BLOCKS, T], F32, name="result")
 
         slots, scores, weights, total, shares = {}, {}, {}, {}, {}

@@ -65,11 +65,20 @@ def tile_dependencymemory_kernel(tc, text_table, type_emb, queries, output_mask,
         nc.gpsimd.tensor_copy(away[:], away_wide[:])
         ones = held.tile([TOKENS, P], F32, name="ones")
         nc.gpsimd.memset(ones[:], 1.0)
+        small_identity = held.tile([TOKENS, TOKENS], F32, name="small_identity")
+        make_identity(nc, small_identity[:])
+        mask_diagonal = held.tile([TOKENS, PIECES, TOKENS], F32, name="mask_diagonal")
+        nc.gpsimd.tensor_tensor(
+            mask_diagonal[:],
+            small_identity[:].unsqueeze(1).to_broadcast([TOKENS, PIECES, TOKENS]),
+            mask[0:TOKENS, :].rearrange("p (k i) -> p k i", i=TOKENS),
+            MULT,
+        )
         query_scaled = held.tile([P, BLOCKS, T], F32, name="query_scaled")
         nc.vector.tensor_scalar_mul(query_scaled[:], query[:], 1.0 / math.sqrt(C))
         result = held.tile([P, BLOCKS, T], F32, name="result")
 
-        slots, scores, weights, total, shares = {}, {}, {}, {}, {}
+        slots, scores, total, spread, gain = {}, {}, {}, {}, {}
 
         def look_up(k):
             slots[k] = kept.tile([P, BLOCKS, PIECE], F32, name="slots")
@@ -93,17 +102,19 @@ def tile_dependencymemory_kernel(tc, text_table, type_emb, queries, output_mask,
         def exponentials(k):
             minus_top = work.tile([TOKENS, 1], F32, name="minus_top")
             nc.vector.reduce_max(minus_top[:], scores[k][:], axis=X, negate=True)
-            weights[k] = work.tile([TOKENS, PIECE], F32, name="weights")
+            weights = work.tile([TOKENS, PIECE], F32, name="weights")
             total[k] = work.tile([TOKENS, 1], F32, name="total")
-            nc.scalar.activation(weights[k][:], scores[k][:], EXP, bias=minus_top[:], accum_out=total[k][:])
+            nc.scalar.activation(weights[:], scores[k][:], EXP, bias=minus_top[:], accum_out=total[k][:])
+            spread[k] = kept_psum.tile([P, PIECE], F32, name="spread")
+            nc.tensor.matmul(spread[k][:], ones[:], weights[:], start=True, stop=True)
 
-        def spread(k):
+        def gains(k):
             inverse = work.tile([TOKENS, 1], F32, name="inverse")
             nc.vector.reciprocal(inverse[:], total[k][:])
-            divide = work.tile([TOKENS, P], F32, name="divide")
-            nc.vector.tensor_scalar_mul(divide[:], ones[:], inverse[:])
-            shares[k] = kept_psum.tile([P, PIECE], F32, name="shares")
-            nc.tensor.matmul(shares[k][:], divide[:], weights[k][:], start=True, stop=True)
+            diagonal = work.tile([TOKENS, TOKENS], F32, name="diagonal")
+            nc.scalar.mul(diagonal[:], mask_diagonal[:, k, :], inverse[:])
+            gain[k] = psum.tile([P, TOKENS], F32, name="gain")
+            nc.tensor.matmul(gain[k][:], ones[:], diagonal[:], start=True, stop=True)
 
         def attend(k):
             tokens = slice(k * TOKENS, (k + 1) * TOKENS)
@@ -111,13 +122,13 @@ def tile_dependencymemory_kernel(tc, text_table, type_emb, queries, output_mask,
             nc.vector.tensor_tensor(
                 weighted[:].rearrange("p b t m -> p b (t m)"),
                 slots[k][:],
-                shares[k][:].unsqueeze(1).to_broadcast([P, BLOCKS, PIECE]),
+                spread[k][:].unsqueeze(1).to_broadcast([P, BLOCKS, PIECE]),
                 MULT,
             )
             attended = work.tile([P, BLOCKS, TOKENS], F32, name="attended")
             nc.vector.reduce_sum(attended[:], weighted[:], axis=X)
             nc.vector.tensor_tensor(
-                attended[:], attended[:], mask[:, tokens].unsqueeze(1).to_broadcast([P, BLOCKS, TOKENS]), MULT
+                attended[:], attended[:], gain[k][:].unsqueeze(1).to_broadcast([P, BLOCKS, TOKENS]), MULT
             )
             nc.vector.tensor_tensor(result[:, :, tokens], attended[:], query[:, :, tokens], ADD)
 
@@ -127,7 +138,7 @@ def tile_dependencymemory_kernel(tc, text_table, type_emb, queries, output_mask,
             if 0 <= k - 1 < PIECES:
                 exponentials(k - 1)
             if 0 <= k - 2 < PIECES:
-                spread(k - 2)
+                gains(k - 2)
         for k in range(PIECES):
             attend(k)
 

@@ -43,8 +43,8 @@ def tile_dependencymemory_kernel(tc, text_table, type_emb, queries, output_mask,
         for b in range(BLOCKS):
             nc.sync.dma_start(tables[b][:], text_table[b * P : (b + 1) * P, :])
             nc.sync.dma_start(types[0][:, b, :], type_blocks[:, b, 0:PIECE])
-        mask = held.tile([P, T], F32, name="mask")
-        nc.sync.dma_start(mask[:], output_mask.rearrange("o t -> (o t)").partition_broadcast(P))
+        mask_column = held.tile([TOKENS, PIECES], F32, name="mask_column")
+        nc.sync.dma_start(mask_column[:], output_mask.rearrange("o (k i) -> (o i) k", i=TOKENS))
         for k in range(1, PIECES):
             for b in range(BLOCKS):
                 nc.sync.dma_start(types[k][:, b, :], type_blocks[:, b, k * PIECE : (k + 1) * PIECE])
@@ -63,22 +63,13 @@ def tile_dependencymemory_kernel(tc, text_table, type_emb, queries, output_mask,
         )
         away = held.tile([P, PIECE], BF16, name="away")
         nc.gpsimd.tensor_copy(away[:], away_wide[:])
-        ones = held.tile([TOKENS, P], F32, name="ones")
-        nc.gpsimd.memset(ones[:], 1.0)
-        small_identity = held.tile([TOKENS, TOKENS], F32, name="small_identity")
-        make_identity(nc, small_identity[:])
-        mask_diagonal = held.tile([TOKENS, PIECES, TOKENS], F32, name="mask_diagonal")
-        nc.gpsimd.tensor_tensor(
-            mask_diagonal[:],
-            small_identity[:].unsqueeze(1).to_broadcast([TOKENS, PIECES, TOKENS]),
-            mask[0:TOKENS, :].rearrange("p (k i) -> p k i", i=TOKENS),
-            MULT,
-        )
+        mask_rows = held.tile([TOKENS, PIECES, P], F32, name="mask_rows")
+        nc.scalar.copy(mask_rows[:], mask_column[:].unsqueeze(2).to_broadcast([TOKENS, PIECES, P]))
         query_scaled = held.tile([P, BLOCKS, T], F32, name="query_scaled")
         nc.vector.tensor_scalar_mul(query_scaled[:], query[:], 1.0 / math.sqrt(C))
         result = held.tile([P, BLOCKS, T], F32, name="result")
 
-        slots, scores, total, spread, gain = {}, {}, {}, {}, {}
+        slots, products, scores, weights, total, spread = {}, {}, {}, {}, {}, {}
 
         def look_up(k):
             slots[k] = kept.tile([P, BLOCKS, PIECE], F32, name="slots")
@@ -98,39 +89,32 @@ def tile_dependencymemory_kernel(tc, text_table, type_emb, queries, output_mask,
                     start=False,
                     stop=(b == BLOCKS - 1),
                 )
+            products[k] = kept.tile([P, BLOCKS, TOKENS, M + 1], F32, name="products")
+            nc.scalar.copy(products[k][:, :, :, M : M + 1], query[:, :, k * TOKENS : (k + 1) * TOKENS].unsqueeze(3))
 
         def exponentials(k):
             minus_top = work.tile([TOKENS, 1], F32, name="minus_top")
             nc.vector.reduce_max(minus_top[:], scores[k][:], axis=X, negate=True)
-            weights = work.tile([TOKENS, PIECE], F32, name="weights")
+            weights[k] = work.tile([TOKENS, PIECE], F32, name="weights")
             total[k] = work.tile([TOKENS, 1], F32, name="total")
-            nc.scalar.activation(weights[:], scores[k][:], EXP, bias=minus_top[:], accum_out=total[k][:])
-            spread[k] = kept_psum.tile([P, PIECE], F32, name="spread")
-            nc.tensor.matmul(spread[k][:], ones[:], weights[:], start=True, stop=True)
+            nc.scalar.activation(weights[k][:], scores[k][:], EXP, bias=minus_top[:], accum_out=total[k][:])
 
-        def gains(k):
+        def shares(k):
             inverse = work.tile([TOKENS, 1], F32, name="inverse")
             nc.vector.reciprocal(inverse[:], total[k][:])
-            diagonal = work.tile([TOKENS, TOKENS], F32, name="diagonal")
-            nc.scalar.mul(diagonal[:], mask_diagonal[:, k, :], inverse[:])
-            gain[k] = psum.tile([P, TOKENS], F32, name="gain")
-            nc.tensor.matmul(gain[k][:], ones[:], diagonal[:], start=True, stop=True)
+            gain = work.tile([TOKENS, P], F32, name="gain")
+            nc.scalar.mul(gain[:], mask_rows[:, k, :], inverse[:])
+            spread[k] = kept_psum.tile([P, PIECE], F32, name="spread")
+            nc.tensor.matmul(spread[k][:], gain[:], weights[k][:], start=True, stop=True)
 
         def attend(k):
-            tokens = slice(k * TOKENS, (k + 1) * TOKENS)
-            weighted = work.tile([P, BLOCKS, TOKENS, M], F32, name="weighted")
             nc.vector.tensor_tensor(
-                weighted[:].rearrange("p b t m -> p b (t m)"),
-                slots[k][:],
-                spread[k][:].unsqueeze(1).to_broadcast([P, BLOCKS, PIECE]),
+                products[k][:, :, :, 0:M],
+                slots[k][:].rearrange("p b (t m) -> p b t m", m=M),
+                spread[k][:].rearrange("p (t m) -> p t m", m=M).unsqueeze(1).to_broadcast([P, BLOCKS, TOKENS, M]),
                 MULT,
             )
-            attended = work.tile([P, BLOCKS, TOKENS], F32, name="attended")
-            nc.vector.reduce_sum(attended[:], weighted[:], axis=X)
-            nc.vector.tensor_tensor(
-                attended[:], attended[:], gain[k][:].unsqueeze(1).to_broadcast([P, BLOCKS, TOKENS]), MULT
-            )
-            nc.vector.tensor_tensor(result[:, :, tokens], attended[:], query[:, :, tokens], ADD)
+            nc.vector.reduce_sum(result[:, :, k * TOKENS : (k + 1) * TOKENS], products[k][:], axis=X)
 
         for k in range(PIECES + 2):
             if k < PIECES:
@@ -138,7 +122,7 @@ def tile_dependencymemory_kernel(tc, text_table, type_emb, queries, output_mask,
             if 0 <= k - 1 < PIECES:
                 exponentials(k - 1)
             if 0 <= k - 2 < PIECES:
-                gains(k - 2)
+                shares(k - 2)
         for k in range(PIECES):
             attend(k)
 

@@ -107,13 +107,15 @@ def tile_dependencymemory_kernel(tc, text_table, type_emb, queries, output_mask,
             spread[k] = kept_psum.tile([P, PIECE], F32, name="spread")
             nc.tensor.matmul(spread[k][:], gain[:], weights[k][:], start=True, stop=True)
 
-        def attend(k):
+        def multiply(k):
             nc.vector.tensor_tensor(
                 products[k][:, :, :, 0:M],
                 slots[k][:].rearrange("p b (t m) -> p b t m", m=M),
                 spread[k][:].rearrange("p (t m) -> p t m", m=M).unsqueeze(1).to_broadcast([P, BLOCKS, TOKENS, M]),
                 MULT,
             )
+
+        def add_up(k):
             nc.vector.reduce_sum(result[:, :, k * TOKENS : (k + 1) * TOKENS], products[k][:], axis=X)
 
         for k in range(PIECES + 2):
@@ -123,7 +125,10 @@ def tile_dependencymemory_kernel(tc, text_table, type_emb, queries, output_mask,
                 exponentials(k - 1)
             if 0 <= k - 2 < PIECES:
                 shares(k - 2)
-        for k in range(PIECES):
-            attend(k)
+        for k in range(PIECES + 1):
+            if k < PIECES:
+                multiply(k)
+            if k > 0:
+                add_up(k - 1)
 
         nc.sync.dma_start(out.rearrange("(b p) t -> p b t", p=P), result[:])

@@ -31,7 +31,6 @@ def tile_dependencymemory_kernel(tc, text_table, type_emb, queries, output_mask,
         tc.tile_pool(name="held", bufs=1) as held,
         tc.tile_pool(name="work", bufs=2) as work,
         tc.tile_pool(name="kept", bufs=PIECES) as kept,
-        tc.psum_pool(name="psum", bufs=2) as psum,
         tc.psum_pool(name="kept_psum", bufs=PIECES) as kept_psum,
     ):
         offsets = held.tile([P, N // 16], U16, name="offsets")
@@ -71,10 +70,12 @@ def tile_dependencymemory_kernel(tc, text_table, type_emb, queries, output_mask,
 
         slots, products, scores, weights, total, spread = {}, {}, {}, {}, {}, {}
 
+        for k in range(PIECES):
+            scores[k] = kept_psum.tile([TOKENS, PIECE], F32, name="scores")
+            nc.tensor.matmul(scores[k][:], identity[:, 0:TOKENS], away[:], start=True, stop=False)
+
         def look_up(k):
             slots[k] = kept.tile([P, BLOCKS, PIECE], F32, name="slots")
-            scores[k] = psum.tile([TOKENS, PIECE], F32, name="scores")
-            nc.tensor.matmul(scores[k][:], identity[:, 0:TOKENS], away[:], start=True, stop=False)
             for b in range(BLOCKS):
                 nc.vector.tensor_tensor(
                     slots[k][:, b, :],

@@ -1,14 +1,14 @@
 import math
 
 import concourse.mybir as mybir
-from concourse.masks import make_identity
 
 F32 = mybir.dt.float32
 BF16 = mybir.dt.bfloat16
 U16 = mybir.dt.uint16
 ADD = mybir.AluOpType.add
 MULT = mybir.AluOpType.mult
-IS_GE = mybir.AluOpType.is_ge
+IS_EQUAL = mybir.AluOpType.is_equal
+NOT_EQUAL = mybir.AluOpType.not_equal
 EXP = mybir.ActivationFunctionType.Exp
 X = mybir.AxisListType.X
 
@@ -20,6 +20,7 @@ PIECE = 256
 PIECES = N // PIECE
 TOKENS = PIECE // M
 FAR = -1.0e30
+GPSIMD_PIECE = 1
 
 FLOPS = 4 * C * N
 
@@ -48,20 +49,18 @@ def tile_dependencymemory_kernel(tc, text_table, type_emb, queries, output_mask,
             for b in range(BLOCKS):
                 nc.sync.dma_start(types[k][:, b, :], type_blocks[:, b, k * PIECE : (k + 1) * PIECE])
 
-        identity = held.tile([P, P], BF16, name="identity")
-        make_identity(nc, identity[:])
-        away_wide = held.tile([P, PIECE], F32, name="away_wide")
-        nc.gpsimd.memset(away_wide[:], 0.0)
-        nc.gpsimd.affine_select(
-            out=away_wide[:], in_=away_wide[:], compare_op=IS_GE, fill=FAR,
-            base=0, channel_multiplier=-M, pattern=[[1, PIECE]],
-        )
-        nc.gpsimd.affine_select(
-            out=away_wide[:], in_=away_wide[:], compare_op=IS_GE, fill=FAR,
-            base=M - 1, channel_multiplier=M, pattern=[[-1, PIECE]],
-        )
         away = held.tile([P, PIECE], BF16, name="away")
-        nc.gpsimd.tensor_copy(away[:], away_wide[:])
+        nc.gpsimd.memset(away[:], 0.0)
+        nc.gpsimd.affine_select(
+            out=away[:], in_=away[:], compare_op=IS_EQUAL, fill=FAR,
+            base=0, channel_multiplier=-1, pattern=[[1, TOKENS], [0, M]],
+        )
+        first_rows = held.tile([P, TOKENS], BF16, name="first_rows")
+        nc.gpsimd.memset(first_rows[:], 0.0)
+        nc.gpsimd.affine_select(
+            out=first_rows[:], in_=first_rows[:], compare_op=NOT_EQUAL, fill=1.0,
+            base=0, channel_multiplier=1, pattern=[[-1, TOKENS]],
+        )
         mask_rows = held.tile([TOKENS, PIECES, P], F32, name="mask_rows")
         nc.scalar.copy(mask_rows[:], mask_column[:].unsqueeze(2).to_broadcast([TOKENS, PIECES, P]))
         query_scaled = held.tile([P, BLOCKS, T], F32, name="query_scaled")
@@ -72,26 +71,24 @@ def tile_dependencymemory_kernel(tc, text_table, type_emb, queries, output_mask,
 
         for k in range(PIECES):
             scores[k] = kept_psum.tile([TOKENS, PIECE], F32, name="scores")
-            nc.tensor.matmul(scores[k][:], identity[:, 0:TOKENS], away[:], start=True, stop=False)
+            nc.tensor.matmul(scores[k][:], first_rows[:], away[:], start=True, stop=False)
 
-        def look_up(k):
-            slots[k] = kept.tile([P, BLOCKS, PIECE], F32, name="slots")
-            for b in range(BLOCKS):
-                nc.vector.tensor_tensor(
-                    slots[k][:, b, :],
-                    tables[b][:].indirect(offsets[:, k * (PIECE // 16) : (k + 1) * (PIECE // 16)]),
-                    types[k][:, b, :],
-                    ADD,
-                )
-                nc.tensor.matmul(
-                    scores[k][:],
-                    query_scaled[:, b, k * TOKENS : (k + 1) * TOKENS],
-                    slots[k][:, b, :],
-                    start=False,
-                    stop=(b == BLOCKS - 1),
-                )
-            products[k] = kept.tile([P, BLOCKS, TOKENS, M + 1], F32, name="products")
-            nc.scalar.copy(products[k][:, :, :, M : M + 1], query[:, :, k * TOKENS : (k + 1) * TOKENS].unsqueeze(3))
+        def look_up(k, b):
+            if b == 0:
+                slots[k] = kept.tile([P, BLOCKS, PIECE], F32, name="slots")
+            nc.vector.tensor_tensor(
+                slots[k][:, b, :],
+                tables[b][:].indirect(offsets[:, k * (PIECE // 16) : (k + 1) * (PIECE // 16)]),
+                types[k][:, b, :],
+                ADD,
+            )
+            nc.tensor.matmul(
+                scores[k][:],
+                query_scaled[:, b, k * TOKENS : (k + 1) * TOKENS],
+                slots[k][:, b, :],
+                start=False,
+                stop=(b == BLOCKS - 1),
+            )
 
         def exponentials(k):
             minus_top = work.tile([TOKENS, 1], F32, name="minus_top")
@@ -109,6 +106,8 @@ def tile_dependencymemory_kernel(tc, text_table, type_emb, queries, output_mask,
             nc.tensor.matmul(spread[k][:], gain[:], weights[k][:], start=True, stop=True)
 
         def multiply(k):
+            products[k] = kept.tile([P, BLOCKS, TOKENS, M + 1], F32, name="products")
+            nc.scalar.copy(products[k][:, :, :, M : M + 1], query[:, :, k * TOKENS : (k + 1) * TOKENS].unsqueeze(3))
             nc.vector.tensor_tensor(
                 products[k][:, :, :, 0:M],
                 slots[k][:].rearrange("p b (t m) -> p b t m", m=M),
@@ -119,17 +118,37 @@ def tile_dependencymemory_kernel(tc, text_table, type_emb, queries, output_mask,
         def add_up(k):
             nc.vector.reduce_sum(result[:, :, k * TOKENS : (k + 1) * TOKENS], products[k][:], axis=X)
 
+        def attend_on_gpsimd(k):
+            shares_of_piece = types[PIECES - 1][:, BLOCKS - 1, :]
+            nc.scalar.copy(shares_of_piece, spread[k][:])
+            rows = held.tile([P, BLOCKS, TOKENS, M], F32, name="rows")
+            nc.gpsimd.tensor_tensor(
+                rows[:],
+                slots[k][:].rearrange("p b (t m) -> p b t m", m=M),
+                shares_of_piece.rearrange("p (t m) -> p t m", m=M).unsqueeze(1).to_broadcast([P, BLOCKS, TOKENS, M]),
+                MULT,
+            )
+            width = M // 2
+            while width >= 1:
+                nc.gpsimd.tensor_tensor(rows[:, :, :, 0:width], rows[:, :, :, 0:width], rows[:, :, :, width : 2 * width], ADD)
+                width //= 2
+            tokens = slice(k * TOKENS, (k + 1) * TOKENS)
+            nc.gpsimd.tensor_tensor(result[:, :, tokens].unsqueeze(3), rows[:, :, :, 0:1], query[:, :, tokens].unsqueeze(3), ADD)
+
         for k in range(PIECES + 2):
-            if k < PIECES:
-                look_up(k)
+            for b in range(BLOCKS):
+                if k < PIECES:
+                    look_up(k, b)
+                if b == BLOCKS // 2 - 1 and 0 <= k - 2 < PIECES:
+                    shares(k - 2)
             if 0 <= k - 1 < PIECES:
                 exponentials(k - 1)
-            if 0 <= k - 2 < PIECES:
-                shares(k - 2)
-        for k in range(PIECES + 1):
-            if k < PIECES:
-                multiply(k)
-            if k > 0:
-                add_up(k - 1)
+        attend_on_gpsimd(GPSIMD_PIECE)
+        vector_pieces = [k for k in range(PIECES) if k != GPSIMD_PIECE]
+        for i in range(len(vector_pieces) + 1):
+            if i < len(vector_pieces):
+                multiply(vector_pieces[i])
+            if i > 0:
+                add_up(vector_pieces[i - 1])
 
         nc.sync.dma_start(out.rearrange("(b p) t -> p b t", p=P), result[:])

@@ -20,7 +20,7 @@ PIECE = 256
 PIECES = N // PIECE
 TOKENS = PIECE // M
 FAR = -1.0e30
-GPSIMD_PIECE = 1
+GPSIMD_PIECE = 0
 
 FLOPS = 4 * C * N
 
@@ -139,10 +139,10 @@ def tile_dependencymemory_kernel(tc, text_table, type_emb, queries, output_mask,
             for b in range(BLOCKS):
                 if k < PIECES:
                     look_up(k, b)
-                if b == BLOCKS // 2 - 1 and 0 <= k - 2 < PIECES:
-                    shares(k - 2)
             if 0 <= k - 1 < PIECES:
                 exponentials(k - 1)
+            if 0 <= k - 2 < PIECES:
+                shares(k - 2)
         attend_on_gpsimd(GPSIMD_PIECE)
         vector_pieces = [k for k in range(PIECES) if k != GPSIMD_PIECE]
         for i in range(len(vector_pieces) + 1):

@@ -20,7 +20,7 @@ PIECE = 256
 PIECES = N // PIECE
 TOKENS = PIECE // M
 FAR = -1.0e30
-GPSIMD_PIECE = 0
+GPSIMD_PIECE = 1
 
 FLOPS = 4 * C * N
 

@@ -43,8 +43,9 @@ def tile_dependencymemory_kernel(tc, text_table, type_emb, queries, output_mask,
         for b in range(BLOCKS):
             nc.sync.dma_start(tables[b][:], text_table[b * P : (b + 1) * P, :])
             nc.sync.dma_start(types[0][:, b, :], type_blocks[:, b, 0:PIECE])
-        mask_column = held.tile([TOKENS, PIECES], F32, name="mask_column")
-        nc.sync.dma_start(mask_column[:], output_mask.rearrange("o (k i) -> (o i) k", i=TOKENS))
+        mask_column = held.tile([P, PIECES], F32, name="mask_column")
+        nc.gpsimd.memset(mask_column[:], 0.0)
+        nc.sync.dma_start(mask_column[0:TOKENS, :], output_mask.rearrange("o (k i) -> (o i) k", i=TOKENS))
         for k in range(1, PIECES):
             for b in range(BLOCKS):
                 nc.sync.dma_start(types[k][:, b, :], type_blocks[:, b, k * PIECE : (k + 1) * PIECE])
@@ -55,23 +56,26 @@ def tile_dependencymemory_kernel(tc, text_table, type_emb, queries, output_mask,
             out=away[:], in_=away[:], compare_op=IS_EQUAL, fill=FAR,
             base=0, channel_multiplier=-1, pattern=[[1, TOKENS], [0, M]],
         )
-        first_rows = held.tile([P, TOKENS], BF16, name="first_rows")
-        nc.gpsimd.memset(first_rows[:], 0.0)
+        same_rows = held.tile([P, P], BF16, name="same_rows")
+        nc.gpsimd.memset(same_rows[:], 0.0)
         nc.gpsimd.affine_select(
-            out=first_rows[:], in_=first_rows[:], compare_op=NOT_EQUAL, fill=1.0,
-            base=0, channel_multiplier=1, pattern=[[-1, TOKENS]],
+            out=same_rows[:], in_=same_rows[:], compare_op=NOT_EQUAL, fill=1.0,
+            base=0, channel_multiplier=1, pattern=[[-1, P]],
         )
-        mask_rows = held.tile([TOKENS, PIECES, P], F32, name="mask_rows")
-        nc.scalar.copy(mask_rows[:], mask_column[:].unsqueeze(2).to_broadcast([TOKENS, PIECES, P]))
-        query_scaled = held.tile([P, BLOCKS, T], F32, name="query_scaled")
-        nc.vector.tensor_scalar_mul(query_scaled[:], query[:], 1.0 / math.sqrt(C))
+        mask_rows = held.tile([P, PIECES, P], F32, name="mask_rows")
+        nc.scalar.copy(mask_rows[:], mask_column[:].unsqueeze(2).to_broadcast([P, PIECES, P]))
+        query_rows = held.tile([P, BLOCKS, PIECES, P], F32, name="query_rows")
+        nc.vector.memset(query_rows[:], 0.0)
+        nc.vector.tensor_scalar_mul(
+            query_rows[:, :, :, 0:TOKENS], query[:].rearrange("p b (k i) -> p b k i", i=TOKENS), 1.0 / math.sqrt(C)
+        )
         result = held.tile([P, BLOCKS, T], F32, name="result")
 
         slots, products, scores, weights, total, spread = {}, {}, {}, {}, {}, {}
 
         for k in range(PIECES):
-            scores[k] = kept_psum.tile([TOKENS, PIECE], F32, name="scores")
-            nc.tensor.matmul(scores[k][:], first_rows[:], away[:], start=True, stop=False)
+            scores[k] = kept_psum.tile([P, PIECE], F32, name="scores")
+            nc.tensor.matmul(scores[k][:], same_rows[:], away[:], start=True, stop=False)
 
         def look_up(k, b):
             if b == 0:
@@ -84,23 +88,23 @@ def tile_dependencymemory_kernel(tc, text_table, type_emb, queries, output_mask,
             )
             nc.tensor.matmul(
                 scores[k][:],
-                query_scaled[:, b, k * TOKENS : (k + 1) * TOKENS],
+                query_rows[:, b, k, :],
                 slots[k][:, b, :],
                 start=False,
                 stop=(b == BLOCKS - 1),
             )
 
         def exponentials(k):
-            minus_top = work.tile([TOKENS, 1], F32, name="minus_top")
+            minus_top = work.tile([P, 1], F32, name="minus_top")
             nc.vector.reduce_max(minus_top[:], scores[k][:], axis=X, negate=True)
-            weights[k] = work.tile([TOKENS, PIECE], F32, name="weights")
-            total[k] = work.tile([TOKENS, 1], F32, name="total")
+            weights[k] = work.tile([P, PIECE], F32, name="weights")
+            total[k] = work.tile([P, 1], F32, name="total")
             nc.scalar.activation(weights[k][:], scores[k][:], EXP, bias=minus_top[:], accum_out=total[k][:])
 
         def shares(k):
-            inverse = work.tile([TOKENS, 1], F32, name="inverse")
+            inverse = work.tile([P, 1], F32, name="inverse")
             nc.vector.reciprocal(inverse[:], total[k][:])
-            gain = work.tile([TOKENS, P], F32, name="gain")
+            gain = work.tile([P, P], F32, name="gain")
             nc.scalar.mul(gain[:], mask_rows[:, k, :], inverse[:])
             spread[k] = kept_psum.tile([P, PIECE], F32, name="spread")
             nc.tensor.matmul(spread[k][:], gain[:], weights[k][:], start=True, stop=True)

@@ -20,7 +20,9 @@ PIECE = 256
 PIECES = N // PIECE
 TOKENS = PIECE // M
 FAR = -1.0e30
-GPSIMD_PIECE = 1
+GPSIMD_PIECE = 0
+EXPONENTIALS_BEHIND = 1
+SHARES_BEHIND = 9
 
 FLOPS = 4 * C * N
 
@@ -139,14 +141,14 @@ def tile_dependencymemory_kernel(tc, text_table, type_emb, queries, output_mask,
             tokens = slice(k * TOKENS, (k + 1) * TOKENS)
             nc.gpsimd.tensor_tensor(result[:, :, tokens].unsqueeze(3), rows[:, :, :, 0:1], query[:, :, tokens].unsqueeze(3), ADD)
 
-        for k in range(PIECES + 2):
-            for b in range(BLOCKS):
-                if k < PIECES:
-                    look_up(k, b)
-            if 0 <= k - 1 < PIECES:
-                exponentials(k - 1)
-            if 0 <= k - 2 < PIECES:
-                shares(k - 2)
+        for i in range(PIECES * BLOCKS + SHARES_BEHIND):
+            if i < PIECES * BLOCKS:
+                look_up(i // BLOCKS, i % BLOCKS)
+            for k in range(PIECES):
+                if i == k * BLOCKS + BLOCKS - 1 + EXPONENTIALS_BEHIND:
+                    exponentials(k)
+                if i == k * BLOCKS + BLOCKS - 1 + SHARES_BEHIND:
+                    shares(k)
         attend_on_gpsimd(GPSIMD_PIECE)
         vector_pieces = [k for k in range(PIECES) if k != GPSIMD_PIECE]
         for i in range(len(vector_pieces) + 1):

@@ -29,7 +29,8 @@ FLOPS = 4 * C * N
 
 def tile_dependencymemory_kernel(tc, text_table, type_emb, queries, output_mask, offs, out):
     nc = tc.nc
-    type_blocks = type_emb.rearrange("(b p) n -> p b n", p=P)
+    table_blocks = text_table.rearrange("(p b) s -> p b s", b=BLOCKS)
+    type_blocks = type_emb.rearrange("(p b) n -> p b n", b=BLOCKS)
     with (
         tc.tile_pool(name="held", bufs=1) as held,
         tc.tile_pool(name="work", bufs=2) as work,
@@ -39,11 +40,11 @@ def tile_dependencymemory_kernel(tc, text_table, type_emb, queries, output_mask,
         offsets = held.tile([P, N // 16], U16, name="offsets")
         nc.sync.dma_start(offsets[:], offs)
         query = held.tile([P, BLOCKS, T], F32, name="query")
-        nc.sync.dma_start(query[:], queries.rearrange("(b p) t -> p b t", p=P))
+        nc.sync.dma_start(query[:], queries.rearrange("(p b) t -> p b t", b=BLOCKS))
         tables = [held.tile([P, S], F32, name=f"table{b}") for b in range(BLOCKS)]
         types = [held.tile([P, BLOCKS, PIECE], F32, name=f"types{k}") for k in range(PIECES)]
         for b in range(BLOCKS):
-            nc.sync.dma_start(tables[b][:], text_table[b * P : (b + 1) * P, :])
+            nc.sync.dma_start(tables[b][:], table_blocks[:, b, :])
             nc.sync.dma_start(types[0][:, b, :], type_blocks[:, b, 0:PIECE])
         mask_column = held.tile([P, PIECES], F32, name="mask_column")
         nc.gpsimd.memset(mask_column[:], 0.0)
@@ -157,4 +158,4 @@ def tile_dependencymemory_kernel(tc, text_table, type_emb, queries, output_mask,
             if i > 0:
                 add_up(vector_pieces[i - 1])
 
-        nc.sync.dma_start(out.rearrange("(b p) t -> p b t", p=P), result[:])
+        nc.sync.dma_start(out.rearrange("(p b) t -> p b t", b=BLOCKS), result[:])

@@ -20,6 +20,7 @@ PIECE = 256
 PIECES = N // PIECE
 TOKENS = PIECE // M
 FAR = -1.0e30
+ROW = 20
 GPSIMD_PIECE = 0
 EXPONENTIALS_BEHIND = 1
 SHARES_BEHIND = 9
@@ -40,12 +41,13 @@ def tile_dependencymemory_kernel(tc, text_table, type_emb, queries, output_mask,
         offsets = held.tile([P, N // 16], U16, name="offsets")
         nc.sync.dma_start(offsets[:], offs)
         query = held.tile([P, BLOCKS, T], F32, name="query")
-        nc.sync.dma_start(query[:], queries.rearrange("(p b) t -> p b t", b=BLOCKS))
         tables = [held.tile([P, S], F32, name=f"table{b}") for b in range(BLOCKS)]
         types = [held.tile([P, BLOCKS, PIECE], F32, name=f"types{k}") for k in range(PIECES)]
         for b in range(BLOCKS):
             nc.sync.dma_start(tables[b][:], table_blocks[:, b, :])
             nc.sync.dma_start(types[0][:, b, :], type_blocks[:, b, 0:PIECE])
+            if b == 0:
+                nc.sync.dma_start(query[:], queries.rearrange("(p b) t -> p b t", b=BLOCKS))
         mask_column = held.tile([P, PIECES], F32, name="mask_column")
         nc.gpsimd.memset(mask_column[:], 0.0)
         nc.sync.dma_start(mask_column[0:TOKENS, :], output_mask.rearrange("o (k i) -> (o i) k", i=TOKENS))
@@ -113,7 +115,7 @@ def tile_dependencymemory_kernel(tc, text_table, type_emb, queries, output_mask,
             nc.tensor.matmul(spread[k][:], gain[:], weights[k][:], start=True, stop=True)
 
         def multiply(k):
-            products[k] = kept.tile([P, BLOCKS, TOKENS, M + 1], F32, name="products")
+            products[k] = kept.tile([P, BLOCKS, TOKENS, ROW], F32, name="products")
             nc.scalar.copy(products[k][:, :, :, M : M + 1], query[:, :, k * TOKENS : (k + 1) * TOKENS].unsqueeze(3))
             nc.vector.tensor_tensor(
                 products[k][:, :, :, 0:M],
@@ -123,7 +125,7 @@ def tile_dependencymemory_kernel(tc, text_table, type_emb, queries, output_mask,
             )
 
         def add_up(k):
-            nc.vector.reduce_sum(result[:, :, k * TOKENS : (k + 1) * TOKENS], products[k][:], axis=X)
+            nc.vector.reduce_sum(result[:, :, k * TOKENS : (k + 1) * TOKENS], products[k][:, :, :, 0 : M + 1], axis=X)
 
         def attend_on_gpsimd(k):
             shares_of_piece = types[PIECES - 1][:, BLOCKS - 1, :]

@@ -69,11 +69,9 @@ def tile_dependencymemory_kernel(tc, text_table, type_emb, queries, output_mask,
         )
         mask_rows = held.tile([P, PIECES, P], F32, name="mask_rows")
         nc.scalar.copy(mask_rows[:], mask_column[:].unsqueeze(2).to_broadcast([P, PIECES, P]))
-        query_rows = held.tile([P, BLOCKS, PIECES, P], F32, name="query_rows")
-        nc.vector.memset(query_rows[:], 0.0)
-        nc.vector.tensor_scalar_mul(
-            query_rows[:, :, :, 0:TOKENS], query[:].rearrange("p b (k i) -> p b k i", i=TOKENS), 1.0 / math.sqrt(C)
-        )
+        query_wide = held.tile([P, BLOCKS, T + P - TOKENS], F32, name="query_wide")
+        nc.gpsimd.memset(query_wide[:, :, T:], 0.0)
+        nc.vector.tensor_scalar_mul(query_wide[:, :, 0:T], query[:], 1.0 / math.sqrt(C))
         result = held.tile([P, BLOCKS, T], F32, name="result")
 
         slots, products, scores, weights, total, spread = {}, {}, {}, {}, {}, {}
@@ -93,7 +91,7 @@ def tile_dependencymemory_kernel(tc, text_table, type_emb, queries, output_mask,
             )
             nc.tensor.matmul(
                 scores[k][:],
-                query_rows[:, b, k, :],
+                query_wide[:, b, k * TOKENS : k * TOKENS + P],
                 slots[k][:, b, :],
                 start=False,
                 stop=(b == BLOCKS - 1),

import math

import concourse.mybir as mybir

F32 = mybir.dt.float32
BF16 = mybir.dt.bfloat16
U16 = mybir.dt.uint16
ADD = mybir.AluOpType.add
MULT = mybir.AluOpType.mult
IS_EQUAL = mybir.AluOpType.is_equal
NOT_EQUAL = mybir.AluOpType.not_equal
EXP = mybir.ActivationFunctionType.Exp
X = mybir.AxisListType.X

P = 128
C, S, T, M = 512, 256, 64, 16
N = T * M
BLOCKS = C // P
PIECE = 256
PIECES = N // PIECE
TOKENS = PIECE // M
FAR = -1.0e30
ROW = 20
GPSIMD_PIECE = 0
EXPONENTIALS_BEHIND = 1
SHARES_BEHIND = 9

FLOPS = 4 * C * N


def tile_dependencymemory_kernel(tc, text_table, type_emb, queries, output_mask, offs, out):
    nc = tc.nc
    table_blocks = text_table.rearrange("(p b) s -> p b s", b=BLOCKS)
    type_blocks = type_emb.rearrange("(p b) n -> p b n", b=BLOCKS)
    with (
        tc.tile_pool(name="held", bufs=1) as held,
        tc.tile_pool(name="work", bufs=2) as work,
        tc.tile_pool(name="kept", bufs=PIECES) as kept,
        tc.psum_pool(name="kept_psum", bufs=PIECES) as kept_psum,
    ):
        offsets = held.tile([P, N // 16], U16, name="offsets")
        nc.sync.dma_start(offsets[:], offs)
        query = held.tile([P, BLOCKS, T], F32, name="query")
        tables = [held.tile([P, S], F32, name=f"table{b}") for b in range(BLOCKS)]
        types = [held.tile([P, BLOCKS, PIECE], F32, name=f"types{k}") for k in range(PIECES)]
        for b in range(BLOCKS):
            nc.sync.dma_start(tables[b][:], table_blocks[:, b, :])
            nc.sync.dma_start(types[0][:, b, :], type_blocks[:, b, 0:PIECE])
            if b == 0:
                nc.sync.dma_start(query[:], queries.rearrange("(p b) t -> p b t", b=BLOCKS))
        mask_column = held.tile([P, PIECES], F32, name="mask_column")
        nc.gpsimd.memset(mask_column[:], 0.0)
        nc.sync.dma_start(mask_column[0:TOKENS, :], output_mask.rearrange("o (k i) -> (o i) k", i=TOKENS))
        for k in range(1, PIECES):
            for b in range(BLOCKS):
                nc.sync.dma_start(types[k][:, b, :], type_blocks[:, b, k * PIECE : (k + 1) * PIECE])

        away = held.tile([P, PIECE], BF16, name="away")
        nc.gpsimd.memset(away[:], 0.0)
        nc.gpsimd.affine_select(
            out=away[:], in_=away[:], compare_op=IS_EQUAL, fill=FAR,
            base=0, channel_multiplier=-1, pattern=[[1, TOKENS], [0, M]],
        )
        same_rows = held.tile([P, P], BF16, name="same_rows")
        nc.gpsimd.memset(same_rows[:], 0.0)
        nc.gpsimd.affine_select(
            out=same_rows[:], in_=same_rows[:], compare_op=NOT_EQUAL, fill=1.0,
            base=0, channel_multiplier=1, pattern=[[-1, P]],
        )
        mask_rows = held.tile([P, PIECES, P], F32, name="mask_rows")
        nc.scalar.copy(mask_rows[:], mask_column[:].unsqueeze(2).to_broadcast([P, PIECES, P]))
        query_wide = held.tile([P, BLOCKS, T + P - TOKENS], F32, name="query_wide")
        nc.gpsimd.memset(query_wide[:, :, T:], 0.0)
        nc.vector.tensor_scalar_mul(query_wide[:, :, 0:T], query[:], 1.0 / math.sqrt(C))
        result = held.tile([P, BLOCKS, T], F32, name="result")

        slots, products, scores, weights, total, spread = {}, {}, {}, {}, {}, {}

        for k in range(PIECES):
            scores[k] = kept_psum.tile([P, PIECE], F32, name="scores")
            nc.tensor.matmul(scores[k][:], same_rows[:], away[:], start=True, stop=False)

        def look_up(k, b):
            if b == 0:
                slots[k] = kept.tile([P, BLOCKS, PIECE], F32, name="slots")
            nc.vector.tensor_tensor(
                slots[k][:, b, :],
                tables[b][:].indirect(offsets[:, k * (PIECE // 16) : (k + 1) * (PIECE // 16)]),
                types[k][:, b, :],
                ADD,
            )
            nc.tensor.matmul(
                scores[k][:],
                query_wide[:, b, k * TOKENS : k * TOKENS + P],
                slots[k][:, b, :],
                start=False,
                stop=(b == BLOCKS - 1),
            )

        def exponentials(k):
            minus_top = work.tile([P, 1], F32, name="minus_top")
            nc.vector.reduce_max(minus_top[:], scores[k][:], axis=X, negate=True)
            weights[k] = work.tile([P, PIECE], F32, name="weights")
            total[k] = work.tile([P, 1], F32, name="total")
            nc.scalar.activation(weights[k][:], scores[k][:], EXP, bias=minus_top[:], accum_out=total[k][:])

        def shares(k):
            inverse = work.tile([P, 1], F32, name="inverse")
            nc.vector.reciprocal(inverse[:], total[k][:])
            gain = work.tile([P, P], F32, name="gain")
            nc.scalar.mul(gain[:], mask_rows[:, k, :], inverse[:])
            spread[k] = kept_psum.tile([P, PIECE], F32, name="spread")
            nc.tensor.matmul(spread[k][:], gain[:], weights[k][:], start=True, stop=True)

        def multiply(k):
            products[k] = kept.tile([P, BLOCKS, TOKENS, ROW], F32, name="products")
            nc.scalar.copy(products[k][:, :, :, M : M + 1], query[:, :, k * TOKENS : (k + 1) * TOKENS].unsqueeze(3))
            nc.vector.tensor_tensor(
                products[k][:, :, :, 0:M],
                slots[k][:].rearrange("p b (t m) -> p b t m", m=M),
                spread[k][:].rearrange("p (t m) -> p t m", m=M).unsqueeze(1).to_broadcast([P, BLOCKS, TOKENS, M]),
                MULT,
            )

        def add_up(k):
            nc.vector.reduce_sum(result[:, :, k * TOKENS : (k + 1) * TOKENS], products[k][:, :, :, 0 : M + 1], axis=X)

        def attend_on_gpsimd(k):
            shares_of_piece = types[PIECES - 1][:, BLOCKS - 1, :]
            nc.scalar.copy(shares_of_piece, spread[k][:])
            rows = held.tile([P, BLOCKS, TOKENS, M], F32, name="rows")
            nc.gpsimd.tensor_tensor(
                rows[:],
                slots[k][:].rearrange("p b (t m) -> p b t m", m=M),
                shares_of_piece.rearrange("p (t m) -> p t m", m=M).unsqueeze(1).to_broadcast([P, BLOCKS, TOKENS, M]),
                MULT,
            )
            width = M // 2
            while width >= 1:
                nc.gpsimd.tensor_tensor(rows[:, :, :, 0:width], rows[:, :, :, 0:width], rows[:, :, :, width : 2 * width], ADD)
                width //= 2
            tokens = slice(k * TOKENS, (k + 1) * TOKENS)
            nc.gpsimd.tensor_tensor(result[:, :, tokens].unsqueeze(3), rows[:, :, :, 0:1], query[:, :, tokens].unsqueeze(3), ADD)

        for i in range(PIECES * BLOCKS + SHARES_BEHIND):
            if i < PIECES * BLOCKS:
                look_up(i // BLOCKS, i % BLOCKS)
            for k in range(PIECES):
                if i == k * BLOCKS + BLOCKS - 1 + EXPONENTIALS_BEHIND:
                    exponentials(k)
                if i == k * BLOCKS + BLOCKS - 1 + SHARES_BEHIND:
                    shares(k)
        attend_on_gpsimd(GPSIMD_PIECE)
        vector_pieces = [k for k in range(PIECES) if k != GPSIMD_PIECE]
        for i in range(len(vector_pieces) + 1):
            if i < len(vector_pieces):
                multiply(vector_pieces[i])
            if i > 0:
                add_up(vector_pieces[i - 1])

        nc.sync.dma_start(out.rearrange("(p b) t -> p b t", b=BLOCKS), result[:])
